import numpy as np
import ml_dtypes


def mxq(x, axis, fmt="e4m3"):
    dtype, down = {"e4m3": (ml_dtypes.float8_e4m3fn, 7), "e5m2": (ml_dtypes.float8_e5m2, 14)}[fmt]
    v = np.moveaxis(np.asarray(x, np.float32).astype(ml_dtypes.bfloat16).astype(np.float64), axis, -1)
    blocks = v.reshape(v.shape[:-1] + (-1, 32))
    amax = np.abs(blocks).max(-1, keepdims=True)
    byte = np.maximum(np.where(amax > 0, np.frexp(amax)[1] - 1 + 127, 0) - down, 1)
    scale = np.exp2(byte - 127.0)
    codes = (blocks / scale).astype(np.float32).astype(dtype).astype(np.float64)
    return np.moveaxis((codes * scale).reshape(v.shape), -1, axis)


WIDE = False


def mx_kscale(k):
    if not WIDE:
        return np.ones(k)
    levels = np.array([10, -10, 5, -5, 0])
    if k % 512:
        return np.exp2(np.random.permutation(np.resize(levels, k // 32))).repeat(32)
    a = np.empty((k // 512, 16))
    for p in range(k // 512):
        a[p, :8] = np.random.permutation(np.resize(levels, 8))
        for g in range(8):
            far = levels[np.abs(levels - a[p, g]) >= 10]
            a[p, g + 8] = far[np.random.randint(len(far))]
    return np.exp2(a.ravel()).repeat(32)


BF16 = ml_dtypes.bfloat16


def bf(x):
    return np.asarray(x, np.float32).astype(BF16)


def f64(x):
    return np.asarray(x).astype(np.float64)


B, N, F, K = 16, 512, 512, 256
BN_EPS = 1e-5
NORM_EPS = 1e-12


def setup_inputs():
    s, t = mx_kscale(N), mx_kscale(F)
    deg = np.random.uniform(0.5, 1.5, size=(B, N, 1))
    return {"x": bf(np.random.standard_normal((B, N, F)) * 0.5 / s[:, None] * t),
            "adj": bf(np.random.uniform(size=(B, N, N)) * deg * 4.0 / np.sqrt(N) * s),
            "W": bf(np.random.standard_normal((F, K)) / np.sqrt(F) / t[:, None]),
            "b": bf(np.random.standard_normal(K) * 0.2)}


def reference(x, adj, W, b):
    agg = mxq(f64(adj), 2, "e4m3") @ mxq(f64(x), 1, "e4m3")
    h = (mxq(agg, 2, "e4m3") @ mxq(f64(W), 0, "e4m3")) + f64(b)
    nrm = np.sqrt(np.sum(h * h, axis=2, keepdims=True))
    h = h / np.maximum(nrm, NORM_EPS)
    h = np.maximum(h, 0.0)
    mean = np.mean(h, axis=(0, 2), keepdims=True)
    var = np.var(h, axis=(0, 2), keepdims=True)
    return (h - mean) / np.sqrt(var + BN_EPS)

@@ -1,0 +1,352 @@
+from contextlib import ExitStack
+
+import concourse.mybir as mybir
+from concourse.masks import make_identity
+
+F32 = mybir.dt.float32
+BF16 = mybir.dt.bfloat16
+U32 = mybir.dt.uint32
+U8 = mybir.dt.uint8
+FP8X4 = mybir.dt.float8_e4m3fn_x4
+ALU = mybir.AluOpType
+ACT = mybir.ActivationFunctionType
+
+P = 128
+PACK = 4
+GRAPHS, NODES, FEATS, OUTS = 16, 512, 512, 256
+NODE_TILES = NODES // P
+FEAT_TILES = FEATS // P
+PAIR = 2
+GROUPS = GRAPHS // PAIR
+UNITS = NODE_TILES * GROUPS
+TRIPLE = 3
+BN_EPS = 1e-5
+NORM_EPS = 1e-12
+
+FLOPS = 2 * GRAPHS * NODES * NODES * FEATS + 2 * GRAPHS * NODES * FEATS * OUTS
+
+LAG_LOAD = 0
+LAG_X_REGROUP = LAG_LOAD + 3
+LAG_X_QUANT = LAG_X_REGROUP + 1
+LAG_TRANSPOSE = LAG_LOAD + 3
+LAG_ADJ_OUT = LAG_TRANSPOSE + 1
+LAG_ADJ_QUANT = LAG_ADJ_OUT + 1
+LAG_AGG = LAG_ADJ_QUANT + 1
+LAG_AGG_OUT = LAG_AGG + 1
+LAG_AGG_QUANT = LAG_AGG_OUT + 1
+LAG_H = LAG_AGG_QUANT + 1
+LAG_BIAS = LAG_H + 1
+LAG_RELU = LAG_BIAS + 1
+LAG_STATS = LAG_RELU + 1
+LAG_NORMS = LAG_RELU + 1
+LAG_MOMENTS = LAG_STATS + 1
+LAG_FACTORS = LAG_MOMENTS + 1
+LAG_APPLY = LAG_FACTORS + GROUPS
+LAG_STORE = LAG_APPLY + 1
+
+
+def tile_routingassignment_pa_t_kernel(tc, x, adj, W, b, out):
+    nc = tc.nc
+    with ExitStack() as ctx:
+
+        def pool(name, bufs):
+            return ctx.enter_context(tc.tile_pool(name=name, bufs=bufs))
+
+        keep = pool("keep", 1)
+        x_raw_pool = pool("x_raw", PAIR * (LAG_X_REGROUP - LAG_LOAD + 1))
+        x_grouped_pool = pool("x_grouped", PAIR * (LAG_X_QUANT - LAG_X_REGROUP + 1))
+        adj_raw_pool = pool("adj_raw", LAG_TRANSPOSE - LAG_LOAD + 1)
+        hand_over = pool("hand_over", 3)
+        result_pool = pool("result", LAG_STORE - LAG_RELU + 1)
+        unread_pool = pool("unread", 4)
+        per_node_tile = pool("per_node_tile", 2)
+        psum_words = ctx.enter_context(tc.psum_pool(name="psum_words", bufs=2))
+        psum_agg = ctx.enter_context(tc.psum_pool(name="psum_agg", bufs=2 * PAIR))
+        psum_h = ctx.enter_context(tc.psum_pool(name="psum_h", bufs=2))
+
+        x_rows = x.rearrange("g (q j) f -> g q (j f)", j=PACK)
+        adj_rows = adj.rearrange("g (p t) m -> p g t m", t=NODE_TILES)
+        out_rows = out.rearrange("g (p t) k -> p g t k", t=NODE_TILES)
+
+        x_codes = [keep.tile([P, FEATS], U32, align_bytes=64, name="x_codes%d" % g) for g in range(GRAPHS)]
+        x_scales = [keep.tile([P, FEATS], U8, align_bytes=64, name="x_scales%d" % g) for g in range(GRAPHS)]
+        w_codes = keep.tile([P, OUTS], U32, align_bytes=64)
+        w_scales = keep.tile([P, OUTS], U8, align_bytes=64)
+        bias = keep.tile([P, PAIR, OUTS], F32)
+        identity = keep.tile([P, P], F32)
+
+        x_raw, x_grouped = {}, {}
+        adj_raw, word_bank, adj_grouped, adj_codes, adj_scales = {}, {}, {}, {}, {}
+        agg_bank, agg_grouped, agg_codes, agg_scales = {}, {}, {}, {}
+        h_bank, h_sb, result = {}, {}, {}
+        square_sum, relu_stats, inverse_norm, inverse_square = {}, {}, {}, {}
+        mean_var, inverse_deviation, factor, shift = {}, {}, {}, {}
+
+        def graphs_of(unit):
+            first = (unit % GROUPS) * PAIR
+            return range(first, first + PAIR)
+
+        def is_last_of_node_tile(unit):
+            return unit % GROUPS == GROUPS - 1
+
+        def prepare_constants():
+            w_raw = keep.tile([P, FEAT_TILES, OUTS], BF16)
+            nc.scalar.dma_start(out=w_raw[:], in_=W.rearrange("(c t) k -> c t k", t=FEAT_TILES))
+            bias_row = keep.tile([P, OUTS], BF16)
+            nc.gpsimd.memset(bias_row[:], 0.0)
+            nc.scalar.dma_start(out=bias_row[0:1, :], in_=b.rearrange("(o k) -> o k", o=1))
+            ones = keep.tile([P, P], BF16)
+            nc.gpsimd.memset(ones[:], 1.0)
+            make_identity(nc, identity[:])
+
+            one = keep.tile([P, 1], F32)
+            nc.gpsimd.memset(one[:], 1.0)
+            nc.scalar.activation(out=one[:], in_=one[:], func=ACT.Abs_reciprocal_sqrt)
+
+            w_grouped = keep.tile([P, OUTS, PACK], BF16, align_bytes=64)
+            nc.vector.tensor_copy(out=w_grouped[:], in_=w_raw[:].rearrange("c t k -> c k t"))
+            nc.vector.quantize_mx(
+                out=w_codes[:].bitcast(FP8X4), scales=w_scales[:], in_=w_grouped[:].rearrange("c k t -> c (k t)")
+            )
+
+            bias_bank = psum_h.tile([P, PAIR, OUTS], F32, name="h_bank")
+            nc.tensor.matmul(out=bias_bank[:, 0, :], lhsT=ones[:], rhs=bias_row[:], start=True, stop=True)
+            for gi in range(PAIR):
+                nc.vector.tensor_copy(out=bias[:, gi, :], in_=bias_bank[:, 0, :])
+
+        def load(unit):
+            node_tile = unit // GROUPS
+            graphs = graphs_of(unit)
+            if node_tile == 0:
+                for g in graphs:
+                    x_raw[g] = x_raw_pool.tile([P, PACK * FEATS], BF16, name="x_raw")
+                    nc.sync.dma_start(out=x_raw[g][:], in_=x_rows[g])
+            adj_raw[unit] = adj_raw_pool.tile([P, PAIR * NODES], BF16, name="adj_raw")
+            nc.sync.dma_start(
+                out=adj_raw[unit][:].rearrange("p (g m) -> p g m", g=PAIR),
+                in_=adj_rows[:, graphs[0] : graphs[0] + PAIR, node_tile, :],
+            )
+
+        def regroup_x(unit):
+            if unit >= GROUPS:
+                return
+            half = P // 2
+            for g in graphs_of(unit):
+                x_grouped[g] = x_grouped_pool.tile([P, FEATS, PACK], BF16, align_bytes=64, name="x_grouped")
+                rows = x_raw[g][:].rearrange("q (j c t) -> q c j t", j=PACK, t=FEAT_TILES)
+                grouped = x_grouped[g][:].rearrange("q (t c) j -> q c j t", t=FEAT_TILES)
+                nc.vector.tensor_copy(out=grouped[:, 0:half], in_=rows[:, 0:half])
+                nc.scalar.copy(out=grouped[:, half:P], in_=rows[:, half:P])
+
+        def quantise_x(unit):
+            if unit >= GROUPS:
+                return
+            for g in graphs_of(unit):
+                nc.vector.quantize_mx(
+                    out=x_codes[g][:].bitcast(FP8X4),
+                    scales=x_scales[g][:],
+                    in_=x_grouped[g][:].rearrange("q f j -> q (f j)"),
+                )
+
+        def transpose_adj(unit):
+            word_bank[unit] = psum_words.tile([P, PAIR, 2, P], F32, name="word_bank")
+            words = adj_raw[unit][:].bitcast(F32)
+            for gi in range(PAIR):
+                for u in range(2):
+                    first = gi * 2 * P
+                    nc.tensor.transpose(
+                        out=word_bank[unit][:, gi, u, :],
+                        in_=words[:, first + u : first + 2 * P : 2],
+                        identity=identity[:],
+                    )
+
+        def copy_adj_out(unit):
+            adj_grouped[unit] = hand_over.tile([P, PAIR * P * PACK], BF16, align_bytes=64, name="adj_grouped")
+            nc.scalar.copy(
+                out=adj_grouped[unit][:].bitcast(F32).rearrange("q (g n u) -> q g n u", g=PAIR, u=2),
+                in_=word_bank[unit][:].rearrange("q g u n -> q g n u"),
+            )
+
+        def quantise_adj(unit):
+            adj_codes[unit] = hand_over.tile([P, PAIR * P], U32, align_bytes=64, name="adj_codes")
+            adj_scales[unit] = hand_over.tile([P, PAIR * P], U8, align_bytes=64, name="adj_scales")
+            nc.vector.quantize_mx(
+                out=adj_codes[unit][:].bitcast(FP8X4), scales=adj_scales[unit][:], in_=adj_grouped[unit][:]
+            )
+
+        def multiply_agg(unit):
+            for gi, g in enumerate(graphs_of(unit)):
+                nodes = slice(gi * P, (gi + 1) * P)
+                agg_bank[unit, gi] = psum_agg.tile([P, FEAT_TILES, P], F32, name="agg_bank")
+                for t in range(FEAT_TILES):
+                    feats = slice(t * P, (t + 1) * P)
+                    nc.tensor.matmul_mx(
+                        out=agg_bank[unit, gi][:, t, :],
+                        lhsT=x_codes[g][:, feats].bitcast(FP8X4),
+                        lhsT_scale=x_scales[g][:, feats],
+                        rhs=adj_codes[unit][:, nodes].bitcast(FP8X4),
+                        rhs_scale=adj_scales[unit][:, nodes],
+                        start=True,
+                        stop=True,
+                    )
+
+        def copy_agg_out(unit):
+            agg_grouped[unit] = hand_over.tile([P, PAIR, P, PACK], BF16, align_bytes=64, name="agg_grouped")
+            for gi in range(PAIR):
+                nc.scalar.copy(
+                    out=agg_grouped[unit][:, gi, :, :], in_=agg_bank[unit, gi][:].rearrange("c t n -> c n t")
+                )
+
+        def quantise_agg(unit):
+            agg_codes[unit] = hand_over.tile([P, PAIR * P], U32, align_bytes=64, name="agg_codes")
+            agg_scales[unit] = hand_over.tile([P, PAIR * P], U8, align_bytes=64, name="agg_scales")
+            nc.vector.quantize_mx(
+                out=agg_codes[unit][:].bitcast(FP8X4),
+                scales=agg_scales[unit][:],
+                in_=agg_grouped[unit][:].rearrange("c g n t -> c (g n t)"),
+            )
+
+        def multiply_h(unit):
+            h_bank[unit] = psum_h.tile([P, PAIR, OUTS], F32, name="h_bank")
+            for gi in range(PAIR):
+                nodes = slice(gi * P, (gi + 1) * P)
+                nc.tensor.matmul_mx(
+                    out=h_bank[unit][:, gi, :],
+                    lhsT=agg_codes[unit][:, nodes].bitcast(FP8X4),
+                    lhsT_scale=agg_scales[unit][:, nodes],
+                    rhs=w_codes[:].bitcast(FP8X4),
+                    rhs_scale=w_scales[:],
+                    start=True,
+                    stop=True,
+                )
+
+        def add_bias(unit):
+            h_sb[unit] = hand_over.tile([P, PAIR, OUTS], F32, name="h_sb")
+            nc.vector.tensor_tensor(out=h_sb[unit][:], in0=h_bank[unit][:], in1=bias[:], op=ALU.add)
+
+        def relu_and_square_sum(unit):
+            node_tile = unit // GROUPS
+            if unit % GROUPS == 0:
+                square_sum[node_tile] = per_node_tile.tile([P, GRAPHS], F32, name="square_sum")
+                relu_stats[node_tile] = per_node_tile.tile([P, GRAPHS, TRIPLE], F32, name="relu_stats")
+            result[unit] = result_pool.tile([P, PAIR, OUTS], F32, name="result")
+            nc.vector.tensor_scalar_max(out=result[unit][:], in0=h_sb[unit][:], scalar1=0.0)
+            for gi, g in enumerate(graphs_of(unit)):
+                squares = unread_pool.tile([P, OUTS], F32, name="squares")
+                nc.scalar.activation(
+                    out=squares[:],
+                    in_=h_sb[unit][:, gi, :],
+                    func=ACT.Square,
+                    accum_out=square_sum[node_tile][:, g : g + 1],
+                )
+
+        def relu_statistics(unit):
+            first = graphs_of(unit)[0]
+            nc.vector.bn_stats(
+                out=relu_stats[unit // GROUPS][:, first : first + PAIR, :].rearrange("p g s -> p (g s)"),
+                in_=result[unit][:].rearrange("p g k -> p k g"),
+            )
+
+        def norms(unit):
+            if not is_last_of_node_tile(unit):
+                return
+            node_tile = unit // GROUPS
+            inverse_norm[node_tile] = per_node_tile.tile([P, GRAPHS], F32, name="inverse_norm")
+            nc.scalar.activation(
+                out=inverse_norm[node_tile][:], in_=square_sum[node_tile][:], func=ACT.Abs_reciprocal_sqrt
+            )
+            clamped = per_node_tile.tile([P, GRAPHS], F32, name="clamped")
+            nc.vector.tensor_scalar_max(out=clamped[:], in0=square_sum[node_tile][:], scalar1=NORM_EPS * NORM_EPS)
+            inverse_square[node_tile] = per_node_tile.tile([P, GRAPHS], F32, name="inverse_square")
+            nc.vector.reciprocal(out=inverse_square[node_tile][:], in_=clamped[:])
+
+        def moments(unit):
+            if not is_last_of_node_tile(unit):
+                return
+            node_tile = unit // GROUPS
+            triples = relu_stats[node_tile]
+            nc.vector.tensor_tensor(
+                out=triples[:, :, 2], in0=triples[:, :, 2], in1=inverse_square[node_tile][:], op=ALU.mult
+            )
+            nc.vector.scalar_tensor_tensor(
+                out=triples[:, :, 1],
+                in0=inverse_norm[node_tile][:],
+                scalar=1.0 / NORM_EPS,
+                in1=triples[:, :, 1],
+                op0=ALU.min,
+                op1=ALU.mult,
+            )
+            mean_var[node_tile] = per_node_tile.tile([P, 2], F32, name="mean_var")
+            nc.vector.bn_aggr(out=mean_var[node_tile][:], in_=triples[:].rearrange("p g s -> p (g s)"))
+            inverse_deviation[node_tile] = per_node_tile.tile([P, 1], F32, name="inverse_deviation")
+            nc.scalar.activation(
+                out=inverse_deviation[node_tile][:],
+                in_=mean_var[node_tile][:, 1:2],
+                func=ACT.Abs_reciprocal_sqrt,
+                bias=BN_EPS,
+            )
+
+        def factors(unit):
+            if not is_last_of_node_tile(unit):
+                return
+            node_tile = unit // GROUPS
+            factor[node_tile] = per_node_tile.tile([P, GRAPHS], F32, name="factor")
+            nc.vector.tensor_scalar(
+                out=factor[node_tile][:],
+                in0=inverse_norm[node_tile][:],
+                scalar1=1.0 / NORM_EPS,
+                scalar2=inverse_deviation[node_tile][:, 0:1],
+                op0=ALU.min,
+                op1=ALU.mult,
+            )
+            shift[node_tile] = per_node_tile.tile([P, 1], F32, name="shift")
+            nc.vector.tensor_scalar(
+                out=shift[node_tile][:],
+                in0=mean_var[node_tile][:, 0:1],
+                scalar1=inverse_deviation[node_tile][:, 0:1],
+                scalar2=-1.0,
+                op0=ALU.mult,
+                op1=ALU.mult,
+            )
+
+        def scale_and_shift(unit):
+            node_tile = unit // GROUPS
+            for gi, g in enumerate(graphs_of(unit)):
+                nc.vector.tensor_scalar(
+                    out=result[unit][:, gi, :],
+                    in0=result[unit][:, gi, :],
+                    scalar1=factor[node_tile][:, g : g + 1],
+                    scalar2=shift[node_tile][:, 0:1],
+                    op0=ALU.mult,
+                    op1=ALU.add,
+                )
+
+        def store(unit):
+            first = graphs_of(unit)[0]
+            nc.sync.dma_start(out=out_rows[:, first : first + PAIR, unit // GROUPS, :], in_=result[unit][:])
+
+        def run(stage, unit):
+            if 0 <= unit < UNITS:
+                stage(unit)
+
+        for step in range(UNITS + LAG_STORE):
+            run(store, step - LAG_STORE)
+            run(scale_and_shift, step - LAG_APPLY)
+            run(factors, step - LAG_FACTORS)
+            run(moments, step - LAG_MOMENTS)
+            run(norms, step - LAG_NORMS)
+            run(relu_statistics, step - LAG_STATS)
+            run(relu_and_square_sum, step - LAG_RELU)
+            run(add_bias, step - LAG_BIAS)
+            run(multiply_h, step - LAG_H)
+            run(quantise_agg, step - LAG_AGG_QUANT)
+            run(copy_agg_out, step - LAG_AGG_OUT)
+            run(multiply_agg, step - LAG_AGG)
+            run(quantise_adj, step - LAG_ADJ_QUANT)
+            run(copy_adj_out, step - LAG_ADJ_OUT)
+            run(transpose_adj, step - LAG_TRANSPOSE)
+            run(quantise_x, step - LAG_X_QUANT)
+            run(regroup_x, step - LAG_X_REGROUP)
+            run(load, step - LAG_LOAD)
+            if step == 0:
+                prepare_constants()

@@ -311,10 +311,22 @@ def tile_routingassignment_pa_t_kernel(tc, x, adj, W, b, out):
 
         def scale_and_shift(unit):
             node_tile = unit // GROUPS
+            is_last_tile = node_tile == NODE_TILES - 1
             for gi, g in enumerate(graphs_of(unit)):
-                nc.vector.tensor_scalar(
-                    out=result[unit][:, gi, :],
-                    in0=result[unit][:, gi, :],
+                values = result[unit][:, gi, :]
+                if is_last_tile and g % 3 == 2:
+                    nc.scalar.activation(
+                        out=values,
+                        in_=values,
+                        func=ACT.Identity,
+                        scale=factor[node_tile][:, g : g + 1],
+                        bias=shift[node_tile][:, 0:1],
+                    )
+                    continue
+                engine = nc.vector if is_last_tile else nc.gpsimd
+                engine.tensor_scalar(
+                    out=values,
+                    in0=values,
                     scalar1=factor[node_tile][:, g : g + 1],
                     scalar2=shift[node_tile][:, 0:1],
                     op0=ALU.mult,

@@ -16,6 +16,7 @@ PACK = 4
 GRAPHS, NODES, FEATS, OUTS = 16, 512, 512, 256
 NODE_TILES = NODES // P
 FEAT_TILES = FEATS // P
+RUN = 8
 PAIR = 2
 GROUPS = GRAPHS // PAIR
 UNITS = NODE_TILES * GROUPS
@@ -91,7 +92,9 @@ def tile_routingassignment_pa_t_kernel(tc, x, adj, W, b, out):
 
         def prepare_constants():
             w_raw = keep.tile([P, FEAT_TILES, OUTS], BF16)
-            nc.scalar.dma_start(out=w_raw[:], in_=W.rearrange("(c t) k -> c t k", t=FEAT_TILES))
+            w_rows = W.rearrange("(b t i) k -> t b i k", t=FEAT_TILES, i=RUN)
+            for t in range(FEAT_TILES):
+                nc.scalar.dma_start(out=w_raw[:, t, :], in_=w_rows[t])
             bias_row = keep.tile([P, OUTS], BF16)
             nc.gpsimd.memset(bias_row[:], 0.0)
             nc.scalar.dma_start(out=bias_row[0:1, :], in_=b.rearrange("(o k) -> o k", o=1))
@@ -130,13 +133,13 @@ def tile_routingassignment_pa_t_kernel(tc, x, adj, W, b, out):
         def regroup_x(unit):
             if unit >= GROUPS:
                 return
-            half = P // 2
             for g in graphs_of(unit):
                 x_grouped[g] = x_grouped_pool.tile([P, FEATS, PACK], BF16, align_bytes=64, name="x_grouped")
-                rows = x_raw[g][:].rearrange("q (j c t) -> q c j t", j=PACK, t=FEAT_TILES)
-                grouped = x_grouped[g][:].rearrange("q (t c) j -> q c j t", t=FEAT_TILES)
-                nc.vector.tensor_copy(out=grouped[:, 0:half], in_=rows[:, 0:half])
-                nc.scalar.copy(out=grouped[:, half:P], in_=rows[:, half:P])
+                rows = x_raw[g][:].rearrange("q (j b t i) -> q t b j i", j=PACK, t=FEAT_TILES, i=RUN)
+                grouped = x_grouped[g][:].rearrange("q (t b i) j -> q t b j i", t=FEAT_TILES, i=RUN)
+                for t in range(FEAT_TILES):
+                    copy = nc.vector.tensor_copy if t < FEAT_TILES // 2 else nc.scalar.copy
+                    copy(out=grouped[:, t], in_=rows[:, t])
 
         def quantise_x(unit):
             if unit >= GROUPS:
@@ -193,9 +196,8 @@ def tile_routingassignment_pa_t_kernel(tc, x, adj, W, b, out):
         def copy_agg_out(unit):
             agg_grouped[unit] = hand_over.tile([P, PAIR, P, PACK], BF16, align_bytes=64, name="agg_grouped")
             for gi in range(PAIR):
-                nc.scalar.copy(
-                    out=agg_grouped[unit][:, gi, :, :], in_=agg_bank[unit, gi][:].rearrange("c t n -> c n t")
-                )
+                copy = nc.vector.tensor_copy if unit % 4 == 3 and gi == PAIR - 1 else nc.scalar.copy
+                copy(out=agg_grouped[unit][:, gi, :, :], in_=agg_bank[unit, gi][:].rearrange("c t n -> c n t"))
 
         def quantise_agg(unit):
             agg_codes[unit] = hand_over.tile([P, PAIR * P], U32, align_bytes=64, name="agg_codes")

@@ -75,6 +75,9 @@ def tile_routingassignment_pa_t_kernel(tc, x, adj, W, b, out):
         w_scales = keep.tile([P, OUTS], U8, align_bytes=64)
         bias = keep.tile([P, PAIR, OUTS], F32)
         identity = keep.tile([P, P], F32)
+        w_raw = keep.tile([P, FEAT_TILES, OUTS], BF16)
+        bias_row = keep.tile([P, OUTS], BF16)
+        ones = keep.tile([P, P], BF16)
 
         x_raw, x_grouped = {}, {}
         adj_raw, word_bank, adj_grouped, adj_codes, adj_scales = {}, {}, {}, {}, {}
@@ -90,15 +93,12 @@ def tile_routingassignment_pa_t_kernel(tc, x, adj, W, b, out):
         def is_last_of_node_tile(unit):
             return unit % GROUPS == GROUPS - 1
 
-        def prepare_constants():
-            w_raw = keep.tile([P, FEAT_TILES, OUTS], BF16)
+        def load_constants():
             w_rows = W.rearrange("(b t i) k -> t b i k", t=FEAT_TILES, i=RUN)
             for t in range(FEAT_TILES):
                 nc.scalar.dma_start(out=w_raw[:, t, :], in_=w_rows[t])
-            bias_row = keep.tile([P, OUTS], BF16)
             nc.gpsimd.memset(bias_row[:], 0.0)
             nc.scalar.dma_start(out=bias_row[0:1, :], in_=b.rearrange("(o k) -> o k", o=1))
-            ones = keep.tile([P, P], BF16)
             nc.gpsimd.memset(ones[:], 1.0)
             make_identity(nc, identity[:])
 
@@ -106,6 +106,7 @@ def tile_routingassignment_pa_t_kernel(tc, x, adj, W, b, out):
             nc.gpsimd.memset(one[:], 1.0)
             nc.scalar.activation(out=one[:], in_=one[:], func=ACT.Abs_reciprocal_sqrt)
 
+        def prepare_w_and_bias():
             w_grouped = keep.tile([P, OUTS, PACK], BF16, align_bytes=64)
             nc.vector.tensor_copy(out=w_grouped[:], in_=w_raw[:].rearrange("c t k -> c k t"))
             nc.vector.quantize_mx(
@@ -343,6 +344,7 @@ def tile_routingassignment_pa_t_kernel(tc, x, adj, W, b, out):
             if 0 <= unit < UNITS:
                 stage(unit)
 
+        ctx.enter_context(tc.manual_schedule())
         for step in range(UNITS + LAG_STORE):
             run(store, step - LAG_STORE)
             run(scale_and_shift, step - LAG_APPLY)
@@ -363,4 +365,6 @@ def tile_routingassignment_pa_t_kernel(tc, x, adj, W, b, out):
             run(regroup_x, step - LAG_X_REGROUP)
             run(load, step - LAG_LOAD)
             if step == 0:
-                prepare_constants()
+                load_constants()
+            if step == LAG_X_QUANT:
+                prepare_w_and_bias()

@@ -16,7 +16,7 @@ PACK = 4
 GRAPHS, NODES, FEATS, OUTS = 16, 512, 512, 256
 NODE_TILES = NODES // P
 FEAT_TILES = FEATS // P
-RUN = 8
+RUN = 4
 PAIR = 2
 GROUPS = GRAPHS // PAIR
 UNITS = NODE_TILES * GROUPS

@@ -20,6 +20,8 @@ RUN = 4
 PAIR = 2
 GROUPS = GRAPHS // PAIR
 UNITS = NODE_TILES * GROUPS
+X_VECTOR = 5
+LAST_UNITS = 4
 TRIPLE = 3
 BN_EPS = 1e-5
 NORM_EPS = 1e-12
@@ -41,7 +43,8 @@ LAG_RELU = LAG_BIAS + 1
 LAG_STATS = LAG_RELU + 1
 LAG_NORMS = LAG_RELU + 1
 LAG_MOMENTS = LAG_STATS + 1
-LAG_FACTORS = LAG_MOMENTS + 1
+LAG_DEVIATION = LAG_MOMENTS + 1
+LAG_FACTORS = LAG_DEVIATION + 1
 LAG_APPLY = LAG_FACTORS + GROUPS
 LAG_STORE = LAG_APPLY + 1
 
@@ -134,12 +137,12 @@ def tile_routingassignment_pa_t_kernel(tc, x, adj, W, b, out):
         def regroup_x(unit):
             if unit >= GROUPS:
                 return
-            for g in graphs_of(unit):
+            for gi, g in enumerate(graphs_of(unit)):
                 x_grouped[g] = x_grouped_pool.tile([P, FEATS, PACK], BF16, align_bytes=64, name="x_grouped")
                 rows = x_raw[g][:].rearrange("q (j b t i) -> q t b j i", j=PACK, t=FEAT_TILES, i=RUN)
                 grouped = x_grouped[g][:].rearrange("q (t b i) j -> q t b j i", t=FEAT_TILES, i=RUN)
                 for t in range(FEAT_TILES):
-                    copy = nc.vector.tensor_copy if t < FEAT_TILES // 2 else nc.scalar.copy
+                    copy = nc.vector.tensor_copy if gi * FEAT_TILES + t < X_VECTOR else nc.scalar.copy
                     copy(out=grouped[:, t], in_=rows[:, t])
 
         def quantise_x(unit):
@@ -197,7 +200,8 @@ def tile_routingassignment_pa_t_kernel(tc, x, adj, W, b, out):
         def copy_agg_out(unit):
             agg_grouped[unit] = hand_over.tile([P, PAIR, P, PACK], BF16, align_bytes=64, name="agg_grouped")
             for gi in range(PAIR):
-                copy = nc.vector.tensor_copy if unit % 4 == 3 and gi == PAIR - 1 else nc.scalar.copy
+                on_vector = unit % 3 == 2 and gi == PAIR - 1 and GROUPS <= unit < UNITS - LAST_UNITS
+                copy = nc.vector.tensor_copy if on_vector else nc.scalar.copy
                 copy(out=agg_grouped[unit][:, gi, :, :], in_=agg_bank[unit, gi][:].rearrange("c t n -> c n t"))
 
         def quantise_agg(unit):
@@ -233,7 +237,10 @@ def tile_routingassignment_pa_t_kernel(tc, x, adj, W, b, out):
                 square_sum[node_tile] = per_node_tile.tile([P, GRAPHS], F32, name="square_sum")
                 relu_stats[node_tile] = per_node_tile.tile([P, GRAPHS, TRIPLE], F32, name="relu_stats")
             result[unit] = result_pool.tile([P, PAIR, OUTS], F32, name="result")
-            nc.vector.tensor_scalar_max(out=result[unit][:], in0=h_sb[unit][:], scalar1=0.0)
+            if UNITS - LAST_UNITS <= unit < UNITS - 1:
+                nc.scalar.activation(out=result[unit][:], in_=h_sb[unit][:], func=ACT.Relu)
+            else:
+                nc.vector.tensor_scalar_max(out=result[unit][:], in0=h_sb[unit][:], scalar1=0.0)
             for gi, g in enumerate(graphs_of(unit)):
                 squares = unread_pool.tile([P, OUTS], F32, name="squares")
                 nc.scalar.activation(
@@ -281,6 +288,11 @@ def tile_routingassignment_pa_t_kernel(tc, x, adj, W, b, out):
             )
             mean_var[node_tile] = per_node_tile.tile([P, 2], F32, name="mean_var")
             nc.vector.bn_aggr(out=mean_var[node_tile][:], in_=triples[:].rearrange("p g s -> p (g s)"))
+
+        def deviation(unit):
+            if not is_last_of_node_tile(unit):
+                return
+            node_tile = unit // GROUPS
             inverse_deviation[node_tile] = per_node_tile.tile([P, 1], F32, name="inverse_deviation")
             nc.scalar.activation(
                 out=inverse_deviation[node_tile][:],
@@ -349,6 +361,7 @@ def tile_routingassignment_pa_t_kernel(tc, x, adj, W, b, out):
             run(store, step - LAG_STORE)
             run(scale_and_shift, step - LAG_APPLY)
             run(factors, step - LAG_FACTORS)
+            run(deviation, step - LAG_DEVIATION)
             run(moments, step - LAG_MOMENTS)
             run(norms, step - LAG_NORMS)
             run(relu_statistics, step - LAG_STATS)

@@ -20,7 +20,7 @@ RUN = 4
 PAIR = 2
 GROUPS = GRAPHS // PAIR
 UNITS = NODE_TILES * GROUPS
-X_VECTOR = 5
+FIRST_TILES = 2
 LAST_UNITS = 4
 TRIPLE = 3
 BN_EPS = 1e-5
@@ -33,11 +33,11 @@ LAG_X_REGROUP = LAG_LOAD + 3
 LAG_X_QUANT = LAG_X_REGROUP + 1
 LAG_TRANSPOSE = LAG_LOAD + 3
 LAG_ADJ_OUT = LAG_TRANSPOSE + 1
-LAG_ADJ_QUANT = LAG_ADJ_OUT + 1
-LAG_AGG = LAG_ADJ_QUANT + 1
+LAG_QUANT_ADJ = LAG_ADJ_OUT + 1
+LAG_AGG = LAG_QUANT_ADJ + 1
 LAG_AGG_OUT = LAG_AGG + 1
-LAG_AGG_QUANT = LAG_AGG_OUT + 1
-LAG_H = LAG_AGG_QUANT + 1
+LAG_QUANT_AGG = LAG_AGG_OUT + 1
+LAG_H = LAG_QUANT_AGG + 1
 LAG_BIAS = LAG_H + 1
 LAG_RELU = LAG_BIAS + 1
 LAG_STATS = LAG_RELU + 1
@@ -45,8 +45,8 @@ LAG_NORMS = LAG_RELU + 1
 LAG_MOMENTS = LAG_STATS + 1
 LAG_DEVIATION = LAG_MOMENTS + 1
 LAG_FACTORS = LAG_DEVIATION + 1
-LAG_APPLY = LAG_FACTORS + GROUPS
-LAG_STORE = LAG_APPLY + 1
+APPLY_RATE = 2
+STEPS = UNITS + LAG_FACTORS + GROUPS // APPLY_RATE
 
 
 def tile_routingassignment_pa_t_kernel(tc, x, adj, W, b, out):
@@ -57,13 +57,13 @@ def tile_routingassignment_pa_t_kernel(tc, x, adj, W, b, out):
             return ctx.enter_context(tc.tile_pool(name=name, bufs=bufs))
 
         keep = pool("keep", 1)
-        x_raw_pool = pool("x_raw", PAIR * (LAG_X_REGROUP - LAG_LOAD + 1))
-        x_grouped_pool = pool("x_grouped", PAIR * (LAG_X_QUANT - LAG_X_REGROUP + 1))
+        x_raw_pool = pool("x_raw", LAG_X_REGROUP - LAG_LOAD + 1)
+        x_grouped_pool = pool("x_grouped", LAG_X_QUANT - LAG_X_REGROUP + 2)
         adj_raw_pool = pool("adj_raw", LAG_TRANSPOSE - LAG_LOAD + 1)
         hand_over = pool("hand_over", 3)
-        result_pool = pool("result", LAG_STORE - LAG_RELU + 1)
+        result_pool = pool("result", FIRST_TILES * GROUPS + LAG_FACTORS - LAG_RELU + 2)
         unread_pool = pool("unread", 4)
-        per_node_tile = pool("per_node_tile", 2)
+        per_node_tile = pool("per_node_tile", NODE_TILES)
         psum_words = ctx.enter_context(tc.psum_pool(name="psum_words", bufs=2))
         psum_agg = ctx.enter_context(tc.psum_pool(name="psum_agg", bufs=2 * PAIR))
         psum_h = ctx.enter_context(tc.psum_pool(name="psum_h", bufs=2))
@@ -76,25 +76,38 @@ def tile_routingassignment_pa_t_kernel(tc, x, adj, W, b, out):
         x_scales = [keep.tile([P, FEATS], U8, align_bytes=64, name="x_scales%d" % g) for g in range(GRAPHS)]
         w_codes = keep.tile([P, OUTS], U32, align_bytes=64)
         w_scales = keep.tile([P, OUTS], U8, align_bytes=64)
-        bias = keep.tile([P, PAIR, OUTS], F32)
+        bias = keep.tile([P, OUTS], F32)
         identity = keep.tile([P, P], F32)
         w_raw = keep.tile([P, FEAT_TILES, OUTS], BF16)
         bias_row = keep.tile([P, OUTS], BF16)
         ones = keep.tile([P, P], BF16)
+        w_grouped = keep.tile([P, OUTS, PACK], BF16, align_bytes=64)
 
         x_raw, x_grouped = {}, {}
-        adj_raw, word_bank, adj_grouped, adj_codes, adj_scales = {}, {}, {}, {}, {}
-        agg_bank, agg_grouped, agg_codes, agg_scales = {}, {}, {}, {}
+        adj_raw, word_bank, grouped, adj_codes, adj_scales = {}, {}, {}, {}, {}
+        agg_bank, agg_codes, agg_scales = {}, {}, {}
         h_bank, h_sb, result = {}, {}, {}
         square_sum, relu_stats, inverse_norm, inverse_square = {}, {}, {}, {}
         mean_var, inverse_deviation, factor, shift = {}, {}, {}, {}
 
+        def node_tile_of(unit):
+            return unit % FIRST_TILES if unit < GRAPHS else unit // GROUPS
+
+        def group_of(unit):
+            return unit // FIRST_TILES if unit < GRAPHS else unit % GROUPS
+
         def graphs_of(unit):
-            first = (unit % GROUPS) * PAIR
+            first = group_of(unit) * PAIR
             return range(first, first + PAIR)
 
         def is_last_of_node_tile(unit):
-            return unit % GROUPS == GROUPS - 1
+            return group_of(unit) == GROUPS - 1
+
+        def gpsimd_copy(out, in_):
+            nc.gpsimd.tensor_scalar(out=out, in0=in_, scalar1=1.0, scalar2=0.0, op0=ALU.mult, op1=ALU.add)
+
+        def spare_engine(node_tile):
+            return nc.vector if node_tile == NODE_TILES - 1 else nc.gpsimd
 
         def load_constants():
             w_rows = W.rearrange("(b t i) k -> t b i k", t=FEAT_TILES, i=RUN)
@@ -109,51 +122,48 @@ def tile_routingassignment_pa_t_kernel(tc, x, adj, W, b, out):
             nc.gpsimd.memset(one[:], 1.0)
             nc.scalar.activation(out=one[:], in_=one[:], func=ACT.Abs_reciprocal_sqrt)
 
+            gpsimd_copy(out=w_grouped[:], in_=w_raw[:].rearrange("c t k -> c k t"))
+
         def prepare_w_and_bias():
-            w_grouped = keep.tile([P, OUTS, PACK], BF16, align_bytes=64)
-            nc.vector.tensor_copy(out=w_grouped[:], in_=w_raw[:].rearrange("c t k -> c k t"))
             nc.vector.quantize_mx(
                 out=w_codes[:].bitcast(FP8X4), scales=w_scales[:], in_=w_grouped[:].rearrange("c k t -> c (k t)")
             )
 
             bias_bank = psum_h.tile([P, PAIR, OUTS], F32, name="h_bank")
             nc.tensor.matmul(out=bias_bank[:, 0, :], lhsT=ones[:], rhs=bias_row[:], start=True, stop=True)
-            for gi in range(PAIR):
-                nc.vector.tensor_copy(out=bias[:, gi, :], in_=bias_bank[:, 0, :])
+            nc.vector.tensor_copy(out=bias[:], in_=bias_bank[:, 0, :])
 
         def load(unit):
-            node_tile = unit // GROUPS
             graphs = graphs_of(unit)
-            if node_tile == 0:
-                for g in graphs:
-                    x_raw[g] = x_raw_pool.tile([P, PACK * FEATS], BF16, name="x_raw")
-                    nc.sync.dma_start(out=x_raw[g][:], in_=x_rows[g])
+            if unit < GRAPHS:
+                x_raw[unit] = x_raw_pool.tile([P, PACK * FEATS], BF16, name="x_raw")
+                nc.sync.dma_start(out=x_raw[unit][:], in_=x_rows[unit])
             adj_raw[unit] = adj_raw_pool.tile([P, PAIR * NODES], BF16, name="adj_raw")
             nc.sync.dma_start(
                 out=adj_raw[unit][:].rearrange("p (g m) -> p g m", g=PAIR),
-                in_=adj_rows[:, graphs[0] : graphs[0] + PAIR, node_tile, :],
+                in_=adj_rows[:, graphs[0] : graphs[0] + PAIR, node_tile_of(unit), :],
             )
 
-        def regroup_x(unit):
-            if unit >= GROUPS:
+        def regroup_x(g):
+            if g >= GRAPHS:
                 return
-            for gi, g in enumerate(graphs_of(unit)):
-                x_grouped[g] = x_grouped_pool.tile([P, FEATS, PACK], BF16, align_bytes=64, name="x_grouped")
-                rows = x_raw[g][:].rearrange("q (j b t i) -> q t b j i", j=PACK, t=FEAT_TILES, i=RUN)
-                grouped = x_grouped[g][:].rearrange("q (t b i) j -> q t b j i", t=FEAT_TILES, i=RUN)
-                for t in range(FEAT_TILES):
-                    copy = nc.vector.tensor_copy if gi * FEAT_TILES + t < X_VECTOR else nc.scalar.copy
-                    copy(out=grouped[:, t], in_=rows[:, t])
+            x_grouped[g] = x_grouped_pool.tile([P, FEATS, PACK], BF16, align_bytes=64, name="x_grouped")
+            rows = x_raw[g][:].rearrange("q (j b t i) -> q t b j i", j=PACK, t=FEAT_TILES, i=RUN)
+            grouped = x_grouped[g][:].rearrange("q (t b i) j -> q t b j i", t=FEAT_TILES, i=RUN)
+            second = nc.scalar.copy if g % 4 == 3 else nc.vector.tensor_copy
+            last = gpsimd_copy if g >= PAIR else nc.scalar.copy
+            copies = [nc.vector.tensor_copy, second, nc.scalar.copy, last]
+            for t, copy in enumerate(copies):
+                copy(out=grouped[:, t], in_=rows[:, t])
 
-        def quantise_x(unit):
-            if unit >= GROUPS:
+        def quantise_x(g):
+            if g >= GRAPHS:
                 return
-            for g in graphs_of(unit):
-                nc.vector.quantize_mx(
-                    out=x_codes[g][:].bitcast(FP8X4),
-                    scales=x_scales[g][:],
-                    in_=x_grouped[g][:].rearrange("q f j -> q (f j)"),
-                )
+            nc.vector.quantize_mx(
+                out=x_codes[g][:].bitcast(FP8X4),
+                scales=x_scales[g][:],
+                in_=x_grouped[g][:].rearrange("q f j -> q (f j)"),
+            )
 
         def transpose_adj(unit):
             word_bank[unit] = psum_words.tile([P, PAIR, 2, P], F32, name="word_bank")
@@ -167,19 +177,33 @@ def tile_routingassignment_pa_t_kernel(tc, x, adj, W, b, out):
                         identity=identity[:],
                     )
 
+        def to_quantise(step):
+            if step not in grouped:
+                grouped[step] = hand_over.tile([P, 2, PAIR, P, PACK], BF16, align_bytes=64, name="grouped")
+            return grouped[step]
+
         def copy_adj_out(unit):
-            adj_grouped[unit] = hand_over.tile([P, PAIR * P * PACK], BF16, align_bytes=64, name="adj_grouped")
+            words = to_quantise(unit + LAG_ADJ_OUT)[:].rearrange("q s g n j -> q (s g n j)").bitcast(F32)
             nc.scalar.copy(
-                out=adj_grouped[unit][:].bitcast(F32).rearrange("q (g n u) -> q g n u", g=PAIR, u=2),
+                out=words[:, PAIR * P * 2 : 2 * PAIR * P * 2].rearrange("q (g n u) -> q g n u", g=PAIR, u=2),
                 in_=word_bank[unit][:].rearrange("q g u n -> q g n u"),
             )
 
-        def quantise_adj(unit):
-            adj_codes[unit] = hand_over.tile([P, PAIR * P], U32, align_bytes=64, name="adj_codes")
-            adj_scales[unit] = hand_over.tile([P, PAIR * P], U8, align_bytes=64, name="adj_scales")
+        def quantise(step):
+            agg_unit, adj_unit = step - LAG_QUANT_AGG, step - LAG_QUANT_ADJ
+            first = 0 if 0 <= agg_unit < UNITS else 1
+            last = 1 if 0 <= adj_unit < UNITS else 0
+            if first > last:
+                return
+            codes = hand_over.tile([P, 2, PAIR * P], U32, align_bytes=64, name="codes")
+            scales = hand_over.tile([P, 2, PAIR * P], U8, align_bytes=64, name="scales")
             nc.vector.quantize_mx(
-                out=adj_codes[unit][:].bitcast(FP8X4), scales=adj_scales[unit][:], in_=adj_grouped[unit][:]
+                out=codes[:, first : last + 1, :].rearrange("q s n -> q (s n)").bitcast(FP8X4),
+                scales=scales[:, first : last + 1, :].rearrange("q s n -> q (s n)"),
+                in_=grouped[step - 1][:, first : last + 1].rearrange("q s g n j -> q (s g n j)"),
             )
+            agg_codes[agg_unit], agg_scales[agg_unit] = codes[:, 0, :], scales[:, 0, :]
+            adj_codes[adj_unit], adj_scales[adj_unit] = codes[:, 1, :], scales[:, 1, :]
 
         def multiply_agg(unit):
             for gi, g in enumerate(graphs_of(unit)):
@@ -198,20 +222,11 @@ def tile_routingassignment_pa_t_kernel(tc, x, adj, W, b, out):
                     )
 
         def copy_agg_out(unit):
-            agg_grouped[unit] = hand_over.tile([P, PAIR, P, PACK], BF16, align_bytes=64, name="agg_grouped")
+            agg_grouped = to_quantise(unit + LAG_AGG_OUT)
             for gi in range(PAIR):
-                on_vector = unit % 3 == 2 and gi == PAIR - 1 and GROUPS <= unit < UNITS - LAST_UNITS
+                on_vector = unit % 2 == 1 and gi == PAIR - 1 and GRAPHS <= unit < UNITS - LAST_UNITS
                 copy = nc.vector.tensor_copy if on_vector else nc.scalar.copy
-                copy(out=agg_grouped[unit][:, gi, :, :], in_=agg_bank[unit, gi][:].rearrange("c t n -> c n t"))
-
-        def quantise_agg(unit):
-            agg_codes[unit] = hand_over.tile([P, PAIR * P], U32, align_bytes=64, name="agg_codes")
-            agg_scales[unit] = hand_over.tile([P, PAIR * P], U8, align_bytes=64, name="agg_scales")
-            nc.vector.quantize_mx(
-                out=agg_codes[unit][:].bitcast(FP8X4),
-                scales=agg_scales[unit][:],
-                in_=agg_grouped[unit][:].rearrange("c g n t -> c (g n t)"),
-            )
+                copy(out=agg_grouped[:, 0, gi, :, :], in_=agg_bank[unit, gi][:].rearrange("c t n -> c n t"))
 
         def multiply_h(unit):
             h_bank[unit] = psum_h.tile([P, PAIR, OUTS], F32, name="h_bank")
@@ -229,11 +244,16 @@ def tile_routingassignment_pa_t_kernel(tc, x, adj, W, b, out):
 
         def add_bias(unit):
             h_sb[unit] = hand_over.tile([P, PAIR, OUTS], F32, name="h_sb")
-            nc.vector.tensor_tensor(out=h_sb[unit][:], in0=h_bank[unit][:], in1=bias[:], op=ALU.add)
+            nc.vector.tensor_tensor(
+                out=h_sb[unit][:],
+                in0=h_bank[unit][:],
+                in1=bias[:].unsqueeze(1).to_broadcast([P, PAIR, OUTS]),
+                op=ALU.add,
+            )
 
         def relu_and_square_sum(unit):
-            node_tile = unit // GROUPS
-            if unit % GROUPS == 0:
+            node_tile = node_tile_of(unit)
+            if group_of(unit) == 0:
                 square_sum[node_tile] = per_node_tile.tile([P, GRAPHS], F32, name="square_sum")
                 relu_stats[node_tile] = per_node_tile.tile([P, GRAPHS, TRIPLE], F32, name="relu_stats")
             result[unit] = result_pool.tile([P, PAIR, OUTS], F32, name="result")
@@ -253,14 +273,14 @@ def tile_routingassignment_pa_t_kernel(tc, x, adj, W, b, out):
         def relu_statistics(unit):
             first = graphs_of(unit)[0]
             nc.vector.bn_stats(
-                out=relu_stats[unit // GROUPS][:, first : first + PAIR, :].rearrange("p g s -> p (g s)"),
+                out=relu_stats[node_tile_of(unit)][:, first : first + PAIR, :].rearrange("p g s -> p (g s)"),
                 in_=result[unit][:].rearrange("p g k -> p k g"),
             )
 
         def norms(unit):
             if not is_last_of_node_tile(unit):
                 return
-            node_tile = unit // GROUPS
+            node_tile = node_tile_of(unit)
             inverse_norm[node_tile] = per_node_tile.tile([P, GRAPHS], F32, name="inverse_norm")
             nc.scalar.activation(
                 out=inverse_norm[node_tile][:], in_=square_sum[node_tile][:], func=ACT.Abs_reciprocal_sqrt
@@ -273,7 +293,7 @@ def tile_routingassignment_pa_t_kernel(tc, x, adj, W, b, out):
         def moments(unit):
             if not is_last_of_node_tile(unit):
                 return
-            node_tile = unit // GROUPS
+            node_tile = node_tile_of(unit)
             triples = relu_stats[node_tile]
             nc.vector.tensor_tensor(
                 out=triples[:, :, 2], in0=triples[:, :, 2], in1=inverse_square[node_tile][:], op=ALU.mult
@@ -292,7 +312,7 @@ def tile_routingassignment_pa_t_kernel(tc, x, adj, W, b, out):
         def deviation(unit):
             if not is_last_of_node_tile(unit):
                 return
-            node_tile = unit // GROUPS
+            node_tile = node_tile_of(unit)
             inverse_deviation[node_tile] = per_node_tile.tile([P, 1], F32, name="inverse_deviation")
             nc.scalar.activation(
                 out=inverse_deviation[node_tile][:],
@@ -304,9 +324,9 @@ def tile_routingassignment_pa_t_kernel(tc, x, adj, W, b, out):
         def factors(unit):
             if not is_last_of_node_tile(unit):
                 return
-            node_tile = unit // GROUPS
+            node_tile = node_tile_of(unit)
             factor[node_tile] = per_node_tile.tile([P, GRAPHS], F32, name="factor")
-            nc.vector.tensor_scalar(
+            spare_engine(node_tile).tensor_scalar(
                 out=factor[node_tile][:],
                 in0=inverse_norm[node_tile][:],
                 scalar1=1.0 / NORM_EPS,
@@ -315,7 +335,7 @@ def tile_routingassignment_pa_t_kernel(tc, x, adj, W, b, out):
                 op1=ALU.mult,
             )
             shift[node_tile] = per_node_tile.tile([P, 1], F32, name="shift")
-            nc.vector.tensor_scalar(
+            spare_engine(node_tile).tensor_scalar(
                 out=shift[node_tile][:],
                 in0=mean_var[node_tile][:, 0:1],
                 scalar1=inverse_deviation[node_tile][:, 0:1],
@@ -325,7 +345,7 @@ def tile_routingassignment_pa_t_kernel(tc, x, adj, W, b, out):
             )
 
         def scale_and_shift(unit):
-            node_tile = unit // GROUPS
+            node_tile = node_tile_of(unit)
             is_last_tile = node_tile == NODE_TILES - 1
             for gi, g in enumerate(graphs_of(unit)):
                 values = result[unit][:, gi, :]
@@ -338,8 +358,7 @@ def tile_routingassignment_pa_t_kernel(tc, x, adj, W, b, out):
                         bias=shift[node_tile][:, 0:1],
                     )
                     continue
-                engine = nc.vector if is_last_tile else nc.gpsimd
-                engine.tensor_scalar(
+                spare_engine(node_tile).tensor_scalar(
                     out=values,
                     in0=values,
                     scalar1=factor[node_tile][:, g : g + 1],
@@ -350,34 +369,39 @@ def tile_routingassignment_pa_t_kernel(tc, x, adj, W, b, out):
 
         def store(unit):
             first = graphs_of(unit)[0]
-            nc.sync.dma_start(out=out_rows[:, first : first + PAIR, unit // GROUPS, :], in_=result[unit][:])
+            nc.sync.dma_start(out=out_rows[:, first : first + PAIR, node_tile_of(unit), :], in_=result[unit][:])
 
         def run(stage, unit):
             if 0 <= unit < UNITS:
                 stage(unit)
 
         ctx.enter_context(tc.manual_schedule())
-        for step in range(UNITS + LAG_STORE):
-            run(store, step - LAG_STORE)
-            run(scale_and_shift, step - LAG_APPLY)
+        ready = []
+        for step in range(STEPS):
+            run(load, step - LAG_LOAD)
+            if step == 0:
+                load_constants()
+            for unit in ready[0:APPLY_RATE]:
+                scale_and_shift(unit)
+                store(unit)
+            ready = ready[APPLY_RATE:]
+            if is_last_of_node_tile(step - LAG_FACTORS) and 0 <= step - LAG_FACTORS < UNITS:
+                done = node_tile_of(step - LAG_FACTORS)
+                ready = ready + [unit for unit in range(UNITS) if node_tile_of(unit) == done]
             run(factors, step - LAG_FACTORS)
             run(deviation, step - LAG_DEVIATION)
             run(moments, step - LAG_MOMENTS)
             run(norms, step - LAG_NORMS)
-            run(relu_statistics, step - LAG_STATS)
             run(relu_and_square_sum, step - LAG_RELU)
+            run(relu_statistics, step - LAG_STATS)
             run(add_bias, step - LAG_BIAS)
             run(multiply_h, step - LAG_H)
-            run(quantise_agg, step - LAG_AGG_QUANT)
+            quantise(step)
             run(copy_agg_out, step - LAG_AGG_OUT)
             run(multiply_agg, step - LAG_AGG)
-            run(quantise_adj, step - LAG_ADJ_QUANT)
             run(copy_adj_out, step - LAG_ADJ_OUT)
             run(transpose_adj, step - LAG_TRANSPOSE)
             run(quantise_x, step - LAG_X_QUANT)
             run(regroup_x, step - LAG_X_REGROUP)
-            run(load, step - LAG_LOAD)
-            if step == 0:
-                load_constants()
-            if step == LAG_X_QUANT:
+            if step == LAG_AGG:
                 prepare_w_and_bias()

from contextlib import ExitStack

import concourse.mybir as mybir
from concourse.masks import make_identity

F32 = mybir.dt.float32
BF16 = mybir.dt.bfloat16
U32 = mybir.dt.uint32
U8 = mybir.dt.uint8
FP8X4 = mybir.dt.float8_e4m3fn_x4
ALU = mybir.AluOpType
ACT = mybir.ActivationFunctionType

P = 128
PACK = 4
GRAPHS, NODES, FEATS, OUTS = 16, 512, 512, 256
NODE_TILES = NODES // P
FEAT_TILES = FEATS // P
RUN = 4
PAIR = 2
GROUPS = GRAPHS // PAIR
UNITS = NODE_TILES * GROUPS
FIRST_TILES = 2
LAST_UNITS = 4
TRIPLE = 3
BN_EPS = 1e-5
NORM_EPS = 1e-12

FLOPS = 2 * GRAPHS * NODES * NODES * FEATS + 2 * GRAPHS * NODES * FEATS * OUTS

LAG_LOAD = 0
LAG_X_REGROUP = LAG_LOAD + 3
LAG_X_QUANT = LAG_X_REGROUP + 1
LAG_TRANSPOSE = LAG_LOAD + 3
LAG_ADJ_OUT = LAG_TRANSPOSE + 1
LAG_QUANT_ADJ = LAG_ADJ_OUT + 1
LAG_AGG = LAG_QUANT_ADJ + 1
LAG_AGG_OUT = LAG_AGG + 1
LAG_QUANT_AGG = LAG_AGG_OUT + 1
LAG_H = LAG_QUANT_AGG + 1
LAG_BIAS = LAG_H + 1
LAG_RELU = LAG_BIAS + 1
LAG_STATS = LAG_RELU + 1
LAG_NORMS = LAG_RELU + 1
LAG_MOMENTS = LAG_STATS + 1
LAG_DEVIATION = LAG_MOMENTS + 1
LAG_FACTORS = LAG_DEVIATION + 1
APPLY_RATE = 2
STEPS = UNITS + LAG_FACTORS + GROUPS // APPLY_RATE


def tile_routingassignment_pa_t_kernel(tc, x, adj, W, b, out):
    nc = tc.nc
    with ExitStack() as ctx:

        def pool(name, bufs):
            return ctx.enter_context(tc.tile_pool(name=name, bufs=bufs))

        keep = pool("keep", 1)
        x_raw_pool = pool("x_raw", LAG_X_REGROUP - LAG_LOAD + 1)
        x_grouped_pool = pool("x_grouped", LAG_X_QUANT - LAG_X_REGROUP + 2)
        adj_raw_pool = pool("adj_raw", LAG_TRANSPOSE - LAG_LOAD + 1)
        hand_over = pool("hand_over", 3)
        result_pool = pool("result", FIRST_TILES * GROUPS + LAG_FACTORS - LAG_RELU + 2)
        unread_pool = pool("unread", 4)
        per_node_tile = pool("per_node_tile", NODE_TILES)
        psum_words = ctx.enter_context(tc.psum_pool(name="psum_words", bufs=2))
        psum_agg = ctx.enter_context(tc.psum_pool(name="psum_agg", bufs=2 * PAIR))
        psum_h = ctx.enter_context(tc.psum_pool(name="psum_h", bufs=2))

        x_rows = x.rearrange("g (q j) f -> g q (j f)", j=PACK)
        adj_rows = adj.rearrange("g (p t) m -> p g t m", t=NODE_TILES)
        out_rows = out.rearrange("g (p t) k -> p g t k", t=NODE_TILES)

        x_codes = [keep.tile([P, FEATS], U32, align_bytes=64, name="x_codes%d" % g) for g in range(GRAPHS)]
        x_scales = [keep.tile([P, FEATS], U8, align_bytes=64, name="x_scales%d" % g) for g in range(GRAPHS)]
        w_codes = keep.tile([P, OUTS], U32, align_bytes=64)
        w_scales = keep.tile([P, OUTS], U8, align_bytes=64)
        bias = keep.tile([P, OUTS], F32)
        identity = keep.tile([P, P], F32)
        w_raw = keep.tile([P, FEAT_TILES, OUTS], BF16)
        bias_row = keep.tile([P, OUTS], BF16)
        ones = keep.tile([P, P], BF16)
        w_grouped = keep.tile([P, OUTS, PACK], BF16, align_bytes=64)

        x_raw, x_grouped = {}, {}
        adj_raw, word_bank, grouped, adj_codes, adj_scales = {}, {}, {}, {}, {}
        agg_bank, agg_codes, agg_scales = {}, {}, {}
        h_bank, h_sb, result = {}, {}, {}
        square_sum, relu_stats, inverse_norm, inverse_square = {}, {}, {}, {}
        mean_var, inverse_deviation, factor, shift = {}, {}, {}, {}

        def node_tile_of(unit):
            return unit % FIRST_TILES if unit < GRAPHS else unit // GROUPS

        def group_of(unit):
            return unit // FIRST_TILES if unit < GRAPHS else unit % GROUPS

        def graphs_of(unit):
            first = group_of(unit) * PAIR
            return range(first, first + PAIR)

        def is_last_of_node_tile(unit):
            return group_of(unit) == GROUPS - 1

        def gpsimd_copy(out, in_):
            nc.gpsimd.tensor_scalar(out=out, in0=in_, scalar1=1.0, scalar2=0.0, op0=ALU.mult, op1=ALU.add)

        def spare_engine(node_tile):
            return nc.vector if node_tile == NODE_TILES - 1 else nc.gpsimd

        def load_constants():
            w_rows = W.rearrange("(b t i) k -> t b i k", t=FEAT_TILES, i=RUN)
            for t in range(FEAT_TILES):
                nc.scalar.dma_start(out=w_raw[:, t, :], in_=w_rows[t])
            nc.gpsimd.memset(bias_row[:], 0.0)
            nc.scalar.dma_start(out=bias_row[0:1, :], in_=b.rearrange("(o k) -> o k", o=1))
            nc.gpsimd.memset(ones[:], 1.0)
            make_identity(nc, identity[:])

            one = keep.tile([P, 1], F32)
            nc.gpsimd.memset(one[:], 1.0)
            nc.scalar.activation(out=one[:], in_=one[:], func=ACT.Abs_reciprocal_sqrt)

            gpsimd_copy(out=w_grouped[:], in_=w_raw[:].rearrange("c t k -> c k t"))

        def prepare_w_and_bias():
            nc.vector.quantize_mx(
                out=w_codes[:].bitcast(FP8X4), scales=w_scales[:], in_=w_grouped[:].rearrange("c k t -> c (k t)")
            )

            bias_bank = psum_h.tile([P, PAIR, OUTS], F32, name="h_bank")
            nc.tensor.matmul(out=bias_bank[:, 0, :], lhsT=ones[:], rhs=bias_row[:], start=True, stop=True)
            nc.vector.tensor_copy(out=bias[:], in_=bias_bank[:, 0, :])

        def load(unit):
            graphs = graphs_of(unit)
            if unit < GRAPHS:
                x_raw[unit] = x_raw_pool.tile([P, PACK * FEATS], BF16, name="x_raw")
                nc.sync.dma_start(out=x_raw[unit][:], in_=x_rows[unit])
            adj_raw[unit] = adj_raw_pool.tile([P, PAIR * NODES], BF16, name="adj_raw")
            nc.sync.dma_start(
                out=adj_raw[unit][:].rearrange("p (g m) -> p g m", g=PAIR),
                in_=adj_rows[:, graphs[0] : graphs[0] + PAIR, node_tile_of(unit), :],
            )

        def regroup_x(g):
            if g >= GRAPHS:
                return
            x_grouped[g] = x_grouped_pool.tile([P, FEATS, PACK], BF16, align_bytes=64, name="x_grouped")
            rows = x_raw[g][:].rearrange("q (j b t i) -> q t b j i", j=PACK, t=FEAT_TILES, i=RUN)
            grouped = x_grouped[g][:].rearrange("q (t b i) j -> q t b j i", t=FEAT_TILES, i=RUN)
            second = nc.scalar.copy if g % 4 == 3 else nc.vector.tensor_copy
            last = gpsimd_copy if g >= PAIR else nc.scalar.copy
            copies = [nc.vector.tensor_copy, second, nc.scalar.copy, last]
            for t, copy in enumerate(copies):
                copy(out=grouped[:, t], in_=rows[:, t])

        def quantise_x(g):
            if g >= GRAPHS:
                return
            nc.vector.quantize_mx(
                out=x_codes[g][:].bitcast(FP8X4),
                scales=x_scales[g][:],
                in_=x_grouped[g][:].rearrange("q f j -> q (f j)"),
            )

        def transpose_adj(unit):
            word_bank[unit] = psum_words.tile([P, PAIR, 2, P], F32, name="word_bank")
            words = adj_raw[unit][:].bitcast(F32)
            for gi in range(PAIR):
                for u in range(2):
                    first = gi * 2 * P
                    nc.tensor.transpose(
                        out=word_bank[unit][:, gi, u, :],
                        in_=words[:, first + u : first + 2 * P : 2],
                        identity=identity[:],
                    )

        def to_quantise(step):
            if step not in grouped:
                grouped[step] = hand_over.tile([P, 2, PAIR, P, PACK], BF16, align_bytes=64, name="grouped")
            return grouped[step]

        def copy_adj_out(unit):
            words = to_quantise(unit + LAG_ADJ_OUT)[:].rearrange("q s g n j -> q (s g n j)").bitcast(F32)
            nc.scalar.copy(
                out=words[:, PAIR * P * 2 : 2 * PAIR * P * 2].rearrange("q (g n u) -> q g n u", g=PAIR, u=2),
                in_=word_bank[unit][:].rearrange("q g u n -> q g n u"),
            )

        def quantise(step):
            agg_unit, adj_unit = step - LAG_QUANT_AGG, step - LAG_QUANT_ADJ
            first = 0 if 0 <= agg_unit < UNITS else 1
            last = 1 if 0 <= adj_unit < UNITS else 0
            if first > last:
                return
            codes = hand_over.tile([P, 2, PAIR * P], U32, align_bytes=64, name="codes")
            scales = hand_over.tile([P, 2, PAIR * P], U8, align_bytes=64, name="scales")
            nc.vector.quantize_mx(
                out=codes[:, first : last + 1, :].rearrange("q s n -> q (s n)").bitcast(FP8X4),
                scales=scales[:, first : last + 1, :].rearrange("q s n -> q (s n)"),
                in_=grouped[step - 1][:, first : last + 1].rearrange("q s g n j -> q (s g n j)"),
            )
            agg_codes[agg_unit], agg_scales[agg_unit] = codes[:, 0, :], scales[:, 0, :]
            adj_codes[adj_unit], adj_scales[adj_unit] = codes[:, 1, :], scales[:, 1, :]

        def multiply_agg(unit):
            for gi, g in enumerate(graphs_of(unit)):
                nodes = slice(gi * P, (gi + 1) * P)
                agg_bank[unit, gi] = psum_agg.tile([P, FEAT_TILES, P], F32, name="agg_bank")
                for t in range(FEAT_TILES):
                    feats = slice(t * P, (t + 1) * P)
                    nc.tensor.matmul_mx(
                        out=agg_bank[unit, gi][:, t, :],
                        lhsT=x_codes[g][:, feats].bitcast(FP8X4),
                        lhsT_scale=x_scales[g][:, feats],
                        rhs=adj_codes[unit][:, nodes].bitcast(FP8X4),
                        rhs_scale=adj_scales[unit][:, nodes],
                        start=True,
                        stop=True,
                    )

        def copy_agg_out(unit):
            agg_grouped = to_quantise(unit + LAG_AGG_OUT)
            for gi in range(PAIR):
                on_vector = unit % 2 == 1 and gi == PAIR - 1 and GRAPHS <= unit < UNITS - LAST_UNITS
                copy = nc.vector.tensor_copy if on_vector else nc.scalar.copy
                copy(out=agg_grouped[:, 0, gi, :, :], in_=agg_bank[unit, gi][:].rearrange("c t n -> c n t"))

        def multiply_h(unit):
            h_bank[unit] = psum_h.tile([P, PAIR, OUTS], F32, name="h_bank")
            for gi in range(PAIR):
                nodes = slice(gi * P, (gi + 1) * P)
                nc.tensor.matmul_mx(
                    out=h_bank[unit][:, gi, :],
                    lhsT=agg_codes[unit][:, nodes].bitcast(FP8X4),
                    lhsT_scale=agg_scales[unit][:, nodes],
                    rhs=w_codes[:].bitcast(FP8X4),
                    rhs_scale=w_scales[:],
                    start=True,
                    stop=True,
                )

        def add_bias(unit):
            h_sb[unit] = hand_over.tile([P, PAIR, OUTS], F32, name="h_sb")
            nc.vector.tensor_tensor(
                out=h_sb[unit][:],
                in0=h_bank[unit][:],
                in1=bias[:].unsqueeze(1).to_broadcast([P, PAIR, OUTS]),
                op=ALU.add,
            )

        def relu_and_square_sum(unit):
            node_tile = node_tile_of(unit)
            if group_of(unit) == 0:
                square_sum[node_tile] = per_node_tile.tile([P, GRAPHS], F32, name="square_sum")
                relu_stats[node_tile] = per_node_tile.tile([P, GRAPHS, TRIPLE], F32, name="relu_stats")
            result[unit] = result_pool.tile([P, PAIR, OUTS], F32, name="result")
            if UNITS - LAST_UNITS <= unit < UNITS - 1:
                nc.scalar.activation(out=result[unit][:], in_=h_sb[unit][:], func=ACT.Relu)
            else:
                nc.vector.tensor_scalar_max(out=result[unit][:], in0=h_sb[unit][:], scalar1=0.0)
            for gi, g in enumerate(graphs_of(unit)):
                squares = unread_pool.tile([P, OUTS], F32, name="squares")
                nc.scalar.activation(
                    out=squares[:],
                    in_=h_sb[unit][:, gi, :],
                    func=ACT.Square,
                    accum_out=square_sum[node_tile][:, g : g + 1],
                )

        def relu_statistics(unit):
            first = graphs_of(unit)[0]
            nc.vector.bn_stats(
                out=relu_stats[node_tile_of(unit)][:, first : first + PAIR, :].rearrange("p g s -> p (g s)"),
                in_=result[unit][:].rearrange("p g k -> p k g"),
            )

        def norms(unit):
            if not is_last_of_node_tile(unit):
                return
            node_tile = node_tile_of(unit)
            inverse_norm[node_tile] = per_node_tile.tile([P, GRAPHS], F32, name="inverse_norm")
            nc.scalar.activation(
                out=inverse_norm[node_tile][:], in_=square_sum[node_tile][:], func=ACT.Abs_reciprocal_sqrt
            )
            clamped = per_node_tile.tile([P, GRAPHS], F32, name="clamped")
            nc.vector.tensor_scalar_max(out=clamped[:], in0=square_sum[node_tile][:], scalar1=NORM_EPS * NORM_EPS)
            inverse_square[node_tile] = per_node_tile.tile([P, GRAPHS], F32, name="inverse_square")
            nc.vector.reciprocal(out=inverse_square[node_tile][:], in_=clamped[:])

        def moments(unit):
            if not is_last_of_node_tile(unit):
                return
            node_tile = node_tile_of(unit)
            triples = relu_stats[node_tile]
            nc.vector.tensor_tensor(
                out=triples[:, :, 2], in0=triples[:, :, 2], in1=inverse_square[node_tile][:], op=ALU.mult
            )
            nc.vector.scalar_tensor_tensor(
                out=triples[:, :, 1],
                in0=inverse_norm[node_tile][:],
                scalar=1.0 / NORM_EPS,
                in1=triples[:, :, 1],
                op0=ALU.min,
                op1=ALU.mult,
            )
            mean_var[node_tile] = per_node_tile.tile([P, 2], F32, name="mean_var")
            nc.vector.bn_aggr(out=mean_var[node_tile][:], in_=triples[:].rearrange("p g s -> p (g s)"))

        def deviation(unit):
            if not is_last_of_node_tile(unit):
                return
            node_tile = node_tile_of(unit)
            inverse_deviation[node_tile] = per_node_tile.tile([P, 1], F32, name="inverse_deviation")
            nc.scalar.activation(
                out=inverse_deviation[node_tile][:],
                in_=mean_var[node_tile][:, 1:2],
                func=ACT.Abs_reciprocal_sqrt,
                bias=BN_EPS,
            )

        def factors(unit):
            if not is_last_of_node_tile(unit):
                return
            node_tile = node_tile_of(unit)
            factor[node_tile] = per_node_tile.tile([P, GRAPHS], F32, name="factor")
            spare_engine(node_tile).tensor_scalar(
                out=factor[node_tile][:],
                in0=inverse_norm[node_tile][:],
                scalar1=1.0 / NORM_EPS,
                scalar2=inverse_deviation[node_tile][:, 0:1],
                op0=ALU.min,
                op1=ALU.mult,
            )
            shift[node_tile] = per_node_tile.tile([P, 1], F32, name="shift")
            spare_engine(node_tile).tensor_scalar(
                out=shift[node_tile][:],
                in0=mean_var[node_tile][:, 0:1],
                scalar1=inverse_deviation[node_tile][:, 0:1],
                scalar2=-1.0,
                op0=ALU.mult,
                op1=ALU.mult,
            )

        def scale_and_shift(unit):
            node_tile = node_tile_of(unit)
            is_last_tile = node_tile == NODE_TILES - 1
            for gi, g in enumerate(graphs_of(unit)):
                values = result[unit][:, gi, :]
                if is_last_tile and g % 3 == 2:
                    nc.scalar.activation(
                        out=values,
                        in_=values,
                        func=ACT.Identity,
                        scale=factor[node_tile][:, g : g + 1],
                        bias=shift[node_tile][:, 0:1],
                    )
                    continue
                spare_engine(node_tile).tensor_scalar(
                    out=values,
                    in0=values,
                    scalar1=factor[node_tile][:, g : g + 1],
                    scalar2=shift[node_tile][:, 0:1],
                    op0=ALU.mult,
                    op1=ALU.add,
                )

        def store(unit):
            first = graphs_of(unit)[0]
            nc.sync.dma_start(out=out_rows[:, first : first + PAIR, node_tile_of(unit), :], in_=result[unit][:])

        def run(stage, unit):
            if 0 <= unit < UNITS:
                stage(unit)

        ctx.enter_context(tc.manual_schedule())
        ready = []
        for step in range(STEPS):
            run(load, step - LAG_LOAD)
            if step == 0:
                load_constants()
            for unit in ready[0:APPLY_RATE]:
                scale_and_shift(unit)
                store(unit)
            ready = ready[APPLY_RATE:]
            if is_last_of_node_tile(step - LAG_FACTORS) and 0 <= step - LAG_FACTORS < UNITS:
                done = node_tile_of(step - LAG_FACTORS)
                ready = ready + [unit for unit in range(UNITS) if node_tile_of(unit) == done]
            run(factors, step - LAG_FACTORS)
            run(deviation, step - LAG_DEVIATION)
            run(moments, step - LAG_MOMENTS)
            run(norms, step - LAG_NORMS)
            run(relu_and_square_sum, step - LAG_RELU)
            run(relu_statistics, step - LAG_STATS)
            run(add_bias, step - LAG_BIAS)
            run(multiply_h, step - LAG_H)
            quantise(step)
            run(copy_agg_out, step - LAG_AGG_OUT)
            run(multiply_agg, step - LAG_AGG)
            run(copy_adj_out, step - LAG_ADJ_OUT)
            run(transpose_adj, step - LAG_TRANSPOSE)
            run(quantise_x, step - LAG_X_QUANT)
            run(regroup_x, step - LAG_X_REGROUP)
            if step == LAG_AGG:
                prepare_w_and_bias()
